import numpy as np
import ml_dtypes


def mxq(x, axis, fmt="e4m3"):
    dtype, down = {"e4m3": (ml_dtypes.float8_e4m3fn, 7), "e5m2": (ml_dtypes.float8_e5m2, 14)}[fmt]
    v = np.moveaxis(np.asarray(x, np.float32).astype(ml_dtypes.bfloat16).astype(np.float64), axis, -1)
    blocks = v.reshape(v.shape[:-1] + (-1, 32))
    amax = np.abs(blocks).max(-1, keepdims=True)
    byte = np.maximum(np.where(amax > 0, np.frexp(amax)[1] - 1 + 127, 0) - down, 1)
    scale = np.exp2(byte - 127.0)
    codes = (blocks / scale).astype(np.float32).astype(dtype).astype(np.float64)
    return np.moveaxis((codes * scale).reshape(v.shape), -1, axis)


WIDE = False


def mx_kscale(k):
    if not WIDE:
        return np.ones(k)
    levels = np.array([30, -30])
    if k % 512:
        return np.exp2(np.random.permutation(np.resize(levels, k // 32))).repeat(32)
    a = np.empty((k // 512, 16))
    for p in range(k // 512):
        a[p, :8] = np.random.permutation(np.resize(levels, 8))
        for g in range(8):
            far = levels[np.abs(levels - a[p, g]) >= 10]
            a[p, g + 8] = far[np.random.randint(len(far))]
    return np.exp2(a.ravel()).repeat(32)


BF16 = ml_dtypes.bfloat16


def bf(x):
    return np.asarray(x, np.float32).astype(BF16)


def f64(x):
    return np.asarray(x).astype(np.float64)


B, S, D, H, HD = 4, 128, 2048, 16, 128
E = H * HD
HALF = HD // 2


def rope(t, fc, fs):
    p = t.reshape(B, S, H, HALF, 2)
    tr, ti = p[..., 0], p[..., 1]
    return np.stack([tr * fc - ti * fs, tr * fs + ti * fc], axis=-1).reshape(B, S, H, HD)


def setup_inputs():
    s = mx_kscale(D)
    return {"x": bf(np.random.standard_normal((B, S, D)) * s),
            "freq_cos": bf(np.cos(np.random.standard_normal((S, HALF)))),
            "freq_sin": bf(np.sin(np.random.standard_normal((S, HALF)))),
            "wq": bf(np.random.standard_normal((E, D)) / np.sqrt(D) / s[None, :]),
            "wk": bf(np.random.standard_normal((E, D)) / np.sqrt(D) / s[None, :])}


def reference(x, freq_cos, freq_sin, wq, wk):
    xq = mxq(f64(x), 2, "e5m2")
    q = (xq @ mxq(f64(wq), 1, "e5m2").T).reshape(B, S, H, HD)
    k = (xq @ mxq(f64(wk), 1, "e5m2").T).reshape(B, S, H, HD)
    fc = f64(freq_cos)[None, :, None, :]
    fs = f64(freq_sin)[None, :, None, :]
    q_rot = rope(q, fc, fs).transpose(0, 2, 1, 3)
    k_rot = rope(k, fc, fs).transpose(0, 2, 1, 3)
    return q_rot, k_rot

@@ -1,0 +1,220 @@
+from contextlib import ExitStack
+
+import concourse.mybir as mybir
+from concourse.masks import make_identity
+
+B, S, D, H, HD = 4, 128, 2048, 16, 128
+E = H * HD
+HALF = HD // 2
+FLOPS = 2 * (B * S) * D * (2 * E)
+
+F32 = mybir.dt.float32
+BF16 = mybir.dt.bfloat16
+U32 = mybir.dt.uint32
+U8 = mybir.dt.uint8
+E5X4 = mybir.dt.float8_e5m2_x4
+
+P = 128
+NT = 512
+PASSES = D // 512
+N_TILES = 2 * E // NT
+W_BUFS = 4
+ADD_ON_GPSIMD = True
+
+
+def tile_attention_pa_kernel(tc, x, freq_cos, freq_sin, wq, wk, out_0, out_1):
+    nc = tc.nc
+    mult = mybir.AluOpType.mult
+    add = mybir.AluOpType.add
+
+    with ExitStack() as ctx:
+        const = ctx.enter_context(tc.tile_pool(name="const", bufs=1))
+        wpool = ctx.enter_context(tc.tile_pool(name="wpool", bufs=W_BUFS))
+        gpool = ctx.enter_context(tc.tile_pool(name="gpool", bufs=4))
+        cpool = ctx.enter_context(tc.tile_pool(name="cpool", bufs=3))
+        rpool = ctx.enter_context(tc.tile_pool(name="rpool", bufs=4))
+        tpsum = ctx.enter_context(tc.psum_pool(name="tpsum", bufs=4))
+        mpsum = ctx.enter_context(tc.psum_pool(name="mpsum", bufs=4))
+        ctx.enter_context(tc.manual_schedule())
+
+        cos_raw = const.tile([P, HALF], BF16, name="cos_raw")
+        sin_raw = const.tile([P, HALF], BF16, name="sin_raw")
+        nc.scalar.dma_start(out=cos_raw[:], in_=freq_cos[:, :])
+        nc.scalar.dma_start(out=sin_raw[:], in_=freq_sin[:, :])
+
+        ident = const.tile([P, P], F32, name="ident")
+        make_identity(nc, ident[:])
+        warm = const.tile([P, 1], F32, name="warm")
+        nc.scalar.copy(out=warm[:], in_=ident[:, 0:1])
+
+        xraw = {}
+        wraw = {}
+
+        def load_x(b):
+            t = const.tile([P, D], BF16, name="xraw%d" % b)
+            nc.sync.dma_start(out=t[:], in_=x[b, :, :])
+            xraw[b] = t
+
+        def load_w(q):
+            n, hf = divmod(q, 2)
+            w = wq if n < N_TILES // 2 else wk
+            r0 = (n % (N_TILES // 2)) * NT
+            t = wpool.tile([P, 4, 1024], BF16, tag="wraw")
+            nc.sync.dma_start(
+                out=t[:],
+                in_=w[r0 : r0 + NT, hf * 1024 : (hf + 1) * 1024].rearrange("(r p) k -> p r k", p=P),
+            )
+            wraw[q] = t
+
+        load_x(0)
+        load_x(1)
+        load_w(0)
+        load_w(1)
+        load_x(2)
+        load_x(3)
+        for q in range(2, W_BUFS):
+            load_w(q)
+
+        table = const.tile([P, 2, NT], F32, name="table")
+
+        def build_tables():
+            cos2v = table[:, 0, :].rearrange("p (h j e) -> p h j e", h=4, e=2)
+            sin2v = table[:, 1, :].rearrange("p (h j e) -> p h j e", h=4, e=2)
+            for h in range(4):
+                nc.vector.tensor_copy(out=cos2v[:, h, :, 0], in_=cos_raw[:])
+                nc.vector.tensor_copy(out=cos2v[:, h, :, 1], in_=cos_raw[:])
+                nc.vector.tensor_copy(out=sin2v[:, h, :, 0], in_=sin_raw[:])
+                nc.vector.tensor_scalar(
+                    out=sin2v[:, h, :, 1], in0=sin_raw[:], scalar1=-1.0, scalar2=None, op0=mult
+                )
+
+        xcodes = const.tile([P, B, 512], U32, name="xcodes", align_bytes=64)
+        xscales = const.tile([P, B, 512], U8, name="xscales", align_bytes=64)
+        wcodes = {}
+        wscales = {}
+
+        def unit_source(unit):
+            if unit[0] == "x":
+                words = xraw[unit[1]][:].bitcast(F32)
+                return lambda a, u: words[:, 256 * a + u : 256 * (a + 1) : 2]
+            n, g = unit[1], unit[2]
+            t = wraw[2 * n + g // 2]
+            c0 = 256 * (g % 2)
+            return lambda a, u: t[:, a, :].bitcast(F32)[:, c0 + u : c0 + 256 : 2]
+
+        def transpose_unit(unit):
+            src = unit_source(unit)
+            banks = []
+            for j in range(2):
+                xt = tpsum.tile([P, 512], F32, tag="xt")
+                for a in range(2):
+                    for u in range(2):
+                        c = (2 * a + u) * P
+                        nc.tensor.transpose(xt[:, c : c + P], src(2 * j + a, u), ident[:])
+                banks.append(xt)
+            return banks
+
+        def evacuate_unit(banks):
+            grouped = gpool.tile([P, 2048], BF16, tag="grouped", align_bytes=64)
+            gw = grouped[:].bitcast(F32)
+            for j in range(2):
+                nc.scalar.copy(
+                    out=gw[:, 512 * j : 512 * (j + 1)].rearrange("p (a c u) -> p a c u", a=2, u=2),
+                    in_=banks[j][:].rearrange("p (a u c) -> p a c u", a=2, u=2),
+                )
+            return grouped
+
+        def quantize_unit(unit, grouped):
+            if unit[0] == "x":
+                codes = xcodes[:, unit[1], :]
+                scales = xscales[:, unit[1], :]
+            else:
+                n, g = unit[1], unit[2]
+                if g == 0:
+                    wc = cpool.tile([P, PASSES, NT], U32, tag="wcodes", align_bytes=64)
+                    ws = cpool.tile([P, PASSES, NT], U8, tag="wscales", align_bytes=64)
+                    wcodes[n] = wc
+                    wscales[n] = ws
+                codes = wcodes[n][:, g, :]
+                scales = wscales[n][:, g, :]
+            nc.vector.quantize_mx(out=codes.bitcast(E5X4), scales=scales, in_=grouped[:])
+
+        def mx_group(n, b):
+            acc = mpsum.tile([P, NT], F32, tag="acc")
+            for g in range(PASSES):
+                cols = slice(P * g, P * (g + 1))
+                nc.tensor.matmul_mx(
+                    out=acc[:],
+                    lhsT=xcodes[:, b, cols].bitcast(E5X4),
+                    lhsT_scale=xscales[:, b, cols],
+                    rhs=wcodes[n][:, g, :].bitcast(E5X4),
+                    rhs_scale=wscales[n][:, g, :],
+                    start=(g == 0),
+                    stop=(g == PASSES - 1),
+                )
+            return acc
+
+        def rope_products(acc):
+            prod = rpool.tile([P, 2, NT], F32, tag="prod")
+            nc.vector.tensor_tensor(
+                out=prod[:], in0=acc[:].unsqueeze(1).to_broadcast([P, 2, NT]), in1=table[:], op=mult
+            )
+            return prod
+
+        def rope_sum_store(n, b, prod):
+            r = rpool.tile([P, NT], F32, tag="rot", bufs=6)
+            eng = nc.gpsimd if ADD_ON_GPSIMD else nc.vector
+            eng.tensor_tensor(
+                out=r[:].rearrange("p (n e) -> p n e", e=2),
+                in0=prod[:, 0, :].rearrange("p (n e) -> p n e", e=2),
+                in1=prod[:, 1, :].rearrange("p (n e) -> p n e", e=2)[:, :, ::-1],
+                op=add,
+            )
+            dst = out_0 if n < N_TILES // 2 else out_1
+            h0 = (n % (N_TILES // 2)) * 4
+            nc.sync.dma_start(
+                out=dst[b, h0 : h0 + 4, :, :].rearrange("h s f -> s h f"),
+                in_=r[:].rearrange("p (h f) -> p h f", h=4),
+            )
+
+        steps = [
+            [("x", 0), ("x", 1)],
+            [("w", 0, 0), ("w", 0, 1)],
+            [("w", 0, 2), ("w", 0, 3)],
+            [("x", 2), ("x", 3)],
+        ]
+        for n in range(1, N_TILES):
+            steps.append([("w", n, 0), ("w", n, 1)])
+            steps.append([("w", n, 2), ("w", n, 3)])
+
+        def groups_after(s):
+            if s < 3:
+                return []
+            if s == 3:
+                return [(0, 0), (0, 1)]
+            if s == 4:
+                return [(0, 2)]
+            if s == 5:
+                return [(0, 3)]
+            n, pair = divmod(s - 4, 2)
+            return [(n, 2 * pair), (n, 2 * pair + 1)]
+
+        next_load = W_BUFS
+        for s in range(len(steps) + 2):
+            units = steps[s] if s < len(steps) else []
+            grouped = []
+            for unit in units:
+                banks = transpose_unit(unit)
+                grouped.append(evacuate_unit(banks))
+            if units and units[0][0] == "w" and next_load < 2 * N_TILES:
+                load_w(next_load)
+                next_load += 1
+            groups = groups_after(s)
+            accs = [mx_group(n, b) for (n, b) in groups]
+            for unit, gr in zip(units, grouped):
+                quantize_unit(unit, gr)
+            if s == 1:
+                build_tables()
+            prods = [rope_products(acc) for acc in accs]
+            for (n, b), pr in zip(groups, prods):
+                rope_sum_store(n, b, pr)

@@ -18,8 +18,13 @@ P = 128
 NT = 512
 PASSES = D // 512
 N_TILES = 2 * E // NT
-W_BUFS = 4
-ADD_ON_GPSIMD = True
+W_BUFS = 6
+
+
+def who_reorders(s, i):
+    if s < 4 or (i == 1 and s % 2 == 0):
+        return None
+    return "S"
 
 
 def tile_attention_pa_kernel(tc, x, freq_cos, freq_sin, wq, wk, out_0, out_1):
@@ -30,9 +35,10 @@ def tile_attention_pa_kernel(tc, x, freq_cos, freq_sin, wq, wk, out_0, out_1):
     with ExitStack() as ctx:
         const = ctx.enter_context(tc.tile_pool(name="const", bufs=1))
         wpool = ctx.enter_context(tc.tile_pool(name="wpool", bufs=W_BUFS))
+        opool = ctx.enter_context(tc.tile_pool(name="opool", bufs=8))
         gpool = ctx.enter_context(tc.tile_pool(name="gpool", bufs=4))
         cpool = ctx.enter_context(tc.tile_pool(name="cpool", bufs=3))
-        rpool = ctx.enter_context(tc.tile_pool(name="rpool", bufs=4))
+        rpool = ctx.enter_context(tc.tile_pool(name="rpool", bufs=6))
         tpsum = ctx.enter_context(tc.psum_pool(name="tpsum", bufs=4))
         mpsum = ctx.enter_context(tc.psum_pool(name="mpsum", bufs=4))
         ctx.enter_context(tc.manual_schedule())
@@ -76,31 +82,42 @@ def tile_attention_pa_kernel(tc, x, freq_cos, freq_sin, wq, wk, out_0, out_1):
             load_w(q)
 
         table = const.tile([P, 2, NT], F32, name="table")
-
-        def build_tables():
-            cos2v = table[:, 0, :].rearrange("p (h j e) -> p h j e", h=4, e=2)
-            sin2v = table[:, 1, :].rearrange("p (h j e) -> p h j e", h=4, e=2)
-            for h in range(4):
-                nc.vector.tensor_copy(out=cos2v[:, h, :, 0], in_=cos_raw[:])
-                nc.vector.tensor_copy(out=cos2v[:, h, :, 1], in_=cos_raw[:])
-                nc.vector.tensor_copy(out=sin2v[:, h, :, 0], in_=sin_raw[:])
-                nc.vector.tensor_scalar(
-                    out=sin2v[:, h, :, 1], in0=sin_raw[:], scalar1=-1.0, scalar2=None, op0=mult
-                )
+        sin2v = table[:, 1, :].rearrange("p (h j e) -> p h j e", h=4, e=2)
+        nc.scalar.copy(
+            out=table[:, 0, :].rearrange("p (h j e) -> p h j e", h=4, e=2),
+            in_=cos_raw[:].unsqueeze(1).unsqueeze(3).to_broadcast([P, 4, HALF, 2]),
+        )
+        nc.scalar.copy(out=sin2v[:, :, :, 0], in_=sin_raw[:].unsqueeze(1).to_broadcast([P, 4, HALF]))
+        nc.scalar.mul(out=sin2v[:, :, :, 1], in_=sin_raw[:].unsqueeze(1).to_broadcast([P, 4, HALF]), mul=-1.0)
 
         xcodes = const.tile([P, B, 512], U32, name="xcodes", align_bytes=64)
         xscales = const.tile([P, B, 512], U8, name="xscales", align_bytes=64)
         wcodes = {}
         wscales = {}
+        ordered = {}
+
+        def unit_words(unit):
+            if unit[0] == "x":
+                return xraw[unit[1]][:].bitcast(F32).rearrange("p (a w) -> p a w", a=4)
+            n, g = unit[1], unit[2]
+            c0 = 256 * (g % 2)
+            return wraw[2 * n + g // 2][:].bitcast(F32)[:, :, c0 : c0 + 256]
+
+        def reorder_unit(unit, who):
+            re = opool.tile([P, 4, 2, P], F32, tag="ordered")
+            src = unit_words(unit).rearrange("p a (m u) -> p a u m", u=2)
+            if who == "S":
+                nc.scalar.copy(out=re[:], in_=src)
+            else:
+                nc.vector.tensor_copy(out=re[:], in_=src)
+            ordered[unit] = re
 
         def unit_source(unit):
-            if unit[0] == "x":
-                words = xraw[unit[1]][:].bitcast(F32)
-                return lambda a, u: words[:, 256 * a + u : 256 * (a + 1) : 2]
-            n, g = unit[1], unit[2]
-            t = wraw[2 * n + g // 2]
-            c0 = 256 * (g % 2)
-            return lambda a, u: t[:, a, :].bitcast(F32)[:, c0 + u : c0 + 256 : 2]
+            if unit in ordered:
+                re = ordered[unit]
+                return lambda a, u: re[:, a, u, :]
+            words = unit_words(unit)
+            return lambda a, u: words[:, a, u:256:2]
 
         def transpose_unit(unit):
             src = unit_source(unit)
@@ -114,14 +131,16 @@ def tile_attention_pa_kernel(tc, x, freq_cos, freq_sin, wq, wk, out_0, out_1):
                 banks.append(xt)
             return banks
 
-        def evacuate_unit(banks):
+        def evacuate_unit(banks, share):
             grouped = gpool.tile([P, 2048], BF16, tag="grouped", align_bytes=64)
             gw = grouped[:].bitcast(F32)
             for j in range(2):
-                nc.scalar.copy(
-                    out=gw[:, 512 * j : 512 * (j + 1)].rearrange("p (a c u) -> p a c u", a=2, u=2),
-                    in_=banks[j][:].rearrange("p (a u c) -> p a c u", a=2, u=2),
-                )
+                dst = gw[:, 512 * j : 512 * (j + 1)].rearrange("p (a c u) -> p a c u", a=2, u=2)
+                src = banks[j][:].rearrange("p (a u c) -> p a c u", a=2, u=2)
+                if share and j == 1:
+                    nc.vector.tensor_copy(out=dst, in_=src)
+                else:
+                    nc.scalar.copy(out=dst, in_=src)
             return grouped
 
         def quantize_unit(unit, grouped):
@@ -138,6 +157,7 @@ def tile_attention_pa_kernel(tc, x, freq_cos, freq_sin, wq, wk, out_0, out_1):
                 codes = wcodes[n][:, g, :]
                 scales = wscales[n][:, g, :]
             nc.vector.quantize_mx(out=codes.bitcast(E5X4), scales=scales, in_=grouped[:])
+            return codes
 
         def mx_group(n, b):
             acc = mpsum.tile([P, NT], F32, tag="acc")
@@ -161,9 +181,8 @@ def tile_attention_pa_kernel(tc, x, freq_cos, freq_sin, wq, wk, out_0, out_1):
             )
             return prod
 
-        def rope_sum_store(n, b, prod):
-            r = rpool.tile([P, NT], F32, tag="rot", bufs=6)
-            eng = nc.gpsimd if ADD_ON_GPSIMD else nc.vector
+        def rope_sum_store(eng, n, b, prod):
+            r = rpool.tile([P, NT], F32, tag="rot")
             eng.tensor_tensor(
                 out=r[:].rearrange("p (n e) -> p n e", e=2),
                 in0=prod[:, 0, :].rearrange("p (n e) -> p n e", e=2),
@@ -186,6 +205,7 @@ def tile_attention_pa_kernel(tc, x, freq_cos, freq_sin, wq, wk, out_0, out_1):
         for n in range(1, N_TILES):
             steps.append([("w", n, 0), ("w", n, 1)])
             steps.append([("w", n, 2), ("w", n, 3)])
+        n_steps = len(steps)
 
         def groups_after(s):
             if s < 3:
@@ -199,13 +219,22 @@ def tile_attention_pa_kernel(tc, x, freq_cos, freq_sin, wq, wk, out_0, out_1):
             n, pair = divmod(s - 4, 2)
             return [(n, 2 * pair), (n, 2 * pair + 1)]
 
+        def reorders(s, who):
+            if 0 <= s < n_steps:
+                for i, unit in enumerate(steps[s]):
+                    if who_reorders(s, i) == who:
+                        reorder_unit(unit, who)
+
         next_load = W_BUFS
-        for s in range(len(steps) + 2):
-            units = steps[s] if s < len(steps) else []
+        reorders(0, "S")
+        for s in range(-1, n_steps + 2):
+            units = steps[s] if 0 <= s < n_steps else []
             grouped = []
             for unit in units:
                 banks = transpose_unit(unit)
-                grouped.append(evacuate_unit(banks))
+                grouped.append(evacuate_unit(banks, s < 4))
+            reorders(s + 2, "S")
+            reorders(s + 1, "V")
             if units and units[0][0] == "w" and next_load < 2 * N_TILES:
                 load_w(next_load)
                 next_load += 1
@@ -213,8 +242,7 @@ def tile_attention_pa_kernel(tc, x, freq_cos, freq_sin, wq, wk, out_0, out_1):
             accs = [mx_group(n, b) for (n, b) in groups]
             for unit, gr in zip(units, grouped):
                 quantize_unit(unit, gr)
-            if s == 1:
-                build_tables()
             prods = [rope_products(acc) for acc in accs]
             for (n, b), pr in zip(groups, prods):
-                rope_sum_store(n, b, pr)
+                last = n == N_TILES - 1 and b == B - 1
+                rope_sum_store(nc.vector if last else nc.gpsimd, n, b, pr)

@@ -27,6 +27,14 @@ def who_reorders(s, i):
     return "S"
 
 
+def add_engine(s, i):
+    if s == 19:
+        return "V"
+    if s == 18:
+        return "G"
+    return "V" if i == 0 else "G"
+
+
 def tile_attention_pa_kernel(tc, x, freq_cos, freq_sin, wq, wk, out_0, out_1):
     nc = tc.nc
     mult = mybir.AluOpType.mult
@@ -50,6 +58,7 @@ def tile_attention_pa_kernel(tc, x, freq_cos, freq_sin, wq, wk, out_0, out_1):
 
         ident = const.tile([P, P], F32, name="ident")
         make_identity(nc, ident[:])
+        junk = const.tile([P, 1], U32, name="junk")
         warm = const.tile([P, 1], F32, name="warm")
         nc.scalar.copy(out=warm[:], in_=ident[:, 0:1])
 
@@ -226,6 +235,7 @@ def tile_attention_pa_kernel(tc, x, freq_cos, freq_sin, wq, wk, out_0, out_1):
                         reorder_unit(unit, who)
 
         next_load = W_BUFS
+        held = []
         reorders(0, "S")
         for s in range(-1, n_steps + 2):
             units = steps[s] if 0 <= s < n_steps else []
@@ -240,9 +250,21 @@ def tile_attention_pa_kernel(tc, x, freq_cos, freq_sin, wq, wk, out_0, out_1):
                 next_load += 1
             groups = groups_after(s)
             accs = [mx_group(n, b) for (n, b) in groups]
+            codes = None
             for unit, gr in zip(units, grouped):
-                quantize_unit(unit, gr)
+                codes = quantize_unit(unit, gr)
+            if codes is not None and held:
+                nc.gpsimd.tensor_copy(out=junk[:], in_=codes[:, 0:1])
+            for (n, b), pr in held:
+                rope_sum_store(nc.gpsimd, n, b, pr)
+            held = []
             prods = [rope_products(acc) for acc in accs]
-            for (n, b), pr in zip(groups, prods):
-                last = n == N_TILES - 1 and b == B - 1
-                rope_sum_store(nc.vector if last else nc.gpsimd, n, b, pr)
+            for i, ((n, b), pr) in enumerate(zip(groups, prods)):
+                if add_engine(s, i) == "V":
+                    rope_sum_store(nc.vector, n, b, pr)
+                else:
+                    held.append(((n, b), pr))
+            if s >= n_steps - 1:
+                for (n, b), pr in held:
+                    rope_sum_store(nc.gpsimd, n, b, pr)
+                held = []

@@ -18,11 +18,11 @@ P = 128
 NT = 512
 PASSES = D // 512
 N_TILES = 2 * E // NT
-W_BUFS = 6
+W_BUFS = 8
 
 
 def who_reorders(s, i):
-    if s < 4 or (i == 1 and s % 2 == 0):
+    if s < 4 or i == 1:
         return None
     return "S"
 
@@ -43,7 +43,7 @@ def tile_attention_pa_kernel(tc, x, freq_cos, freq_sin, wq, wk, out_0, out_1):
     with ExitStack() as ctx:
         const = ctx.enter_context(tc.tile_pool(name="const", bufs=1))
         wpool = ctx.enter_context(tc.tile_pool(name="wpool", bufs=W_BUFS))
-        opool = ctx.enter_context(tc.tile_pool(name="opool", bufs=8))
+        opool = ctx.enter_context(tc.tile_pool(name="opool", bufs=4))
         gpool = ctx.enter_context(tc.tile_pool(name="gpool", bufs=4))
         cpool = ctx.enter_context(tc.tile_pool(name="cpool", bufs=3))
         rpool = ctx.enter_context(tc.tile_pool(name="rpool", bufs=6))
@@ -71,14 +71,11 @@ def tile_attention_pa_kernel(tc, x, freq_cos, freq_sin, wq, wk, out_0, out_1):
             xraw[b] = t
 
         def load_w(q):
-            n, hf = divmod(q, 2)
+            n, rp = divmod(q, 2)
             w = wq if n < N_TILES // 2 else wk
-            r0 = (n % (N_TILES // 2)) * NT
-            t = wpool.tile([P, 4, 1024], BF16, tag="wraw")
-            nc.sync.dma_start(
-                out=t[:],
-                in_=w[r0 : r0 + NT, hf * 1024 : (hf + 1) * 1024].rearrange("(r p) k -> p r k", p=P),
-            )
+            r0 = (n % (N_TILES // 2)) * NT + 256 * rp
+            t = wpool.tile([P, 2, D], BF16, tag="wraw")
+            nc.sync.dma_start(out=t[:], in_=w[r0 : r0 + 256, :].rearrange("(a p) k -> p a k", p=P))
             wraw[q] = t
 
         load_x(0)
@@ -105,16 +102,12 @@ def tile_attention_pa_kernel(tc, x, freq_cos, freq_sin, wq, wk, out_0, out_1):
         wscales = {}
         ordered = {}
 
-        def unit_words(unit):
-            if unit[0] == "x":
-                return xraw[unit[1]][:].bitcast(F32).rearrange("p (a w) -> p a w", a=4)
-            n, g = unit[1], unit[2]
-            c0 = 256 * (g % 2)
-            return wraw[2 * n + g // 2][:].bitcast(F32)[:, :, c0 : c0 + 256]
-
         def reorder_unit(unit, who):
-            re = opool.tile([P, 4, 2, P], F32, tag="ordered")
-            src = unit_words(unit).rearrange("p a (m u) -> p a u m", u=2)
+            n, rp, gp = unit[1], unit[2], unit[3]
+            re = opool.tile([P, 2, 2, 256], F32, tag="ordered")
+            src = wraw[2 * n + rp][:].bitcast(F32)[:, :, 512 * gp : 512 * (gp + 1)].rearrange(
+                "p a (w u) -> p u a w", u=2
+            )
             if who == "S":
                 nc.scalar.copy(out=re[:], in_=src)
             else:
@@ -124,9 +117,15 @@ def tile_attention_pa_kernel(tc, x, freq_cos, freq_sin, wq, wk, out_0, out_1):
         def unit_source(unit):
             if unit in ordered:
                 re = ordered[unit]
-                return lambda a, u: re[:, a, u, :]
-            words = unit_words(unit)
-            return lambda a, u: words[:, a, u:256:2]
+                return lambda j, a, u: re[:, u, a, P * j : P * (j + 1)]
+            if unit[0] == "x":
+                words = xraw[unit[1]][:].bitcast(F32)
+                return lambda j, a, u: words[:, 256 * (2 * j + a) + u : 256 * (2 * j + a + 1) : 2]
+            n, rp, gp = unit[1], unit[2], unit[3]
+            t = wraw[2 * n + rp]
+            return lambda j, a, u: t[:, a, :].bitcast(F32)[
+                :, 256 * (2 * gp + j) + u : 256 * (2 * gp + j + 1) : 2
+            ]
 
         def transpose_unit(unit):
             src = unit_source(unit)
@@ -136,7 +135,7 @@ def tile_attention_pa_kernel(tc, x, freq_cos, freq_sin, wq, wk, out_0, out_1):
                 for a in range(2):
                     for u in range(2):
                         c = (2 * a + u) * P
-                        nc.tensor.transpose(xt[:, c : c + P], src(2 * j + a, u), ident[:])
+                        nc.tensor.transpose(xt[:, c : c + P], src(j, a, u), ident[:])
                 banks.append(xt)
             return banks
 
@@ -155,17 +154,24 @@ def tile_attention_pa_kernel(tc, x, freq_cos, freq_sin, wq, wk, out_0, out_1):
         def quantize_unit(unit, grouped):
             if unit[0] == "x":
                 codes = xcodes[:, unit[1], :]
-                scales = xscales[:, unit[1], :]
-            else:
-                n, g = unit[1], unit[2]
-                if g == 0:
-                    wc = cpool.tile([P, PASSES, NT], U32, tag="wcodes", align_bytes=64)
-                    ws = cpool.tile([P, PASSES, NT], U8, tag="wscales", align_bytes=64)
-                    wcodes[n] = wc
-                    wscales[n] = ws
-                codes = wcodes[n][:, g, :]
-                scales = wscales[n][:, g, :]
-            nc.vector.quantize_mx(out=codes.bitcast(E5X4), scales=scales, in_=grouped[:])
+                nc.vector.quantize_mx(
+                    out=codes.bitcast(E5X4), scales=xscales[:, unit[1], :], in_=grouped[:]
+                )
+                return codes
+            n, rp, gp = unit[1], unit[2], unit[3]
+            if rp == 0 and gp == 0:
+                wc = cpool.tile([P, PASSES, NT], U32, tag="wcodes", align_bytes=64)
+                ws = cpool.tile([P, PASSES, NT], U8, tag="wscales", align_bytes=64)
+                wcodes[n] = wc
+                wscales[n] = ws
+            cols = slice(256 * rp, 256 * (rp + 1))
+            for j in range(2):
+                codes = wcodes[n][:, 2 * gp + j, cols]
+                nc.vector.quantize_mx(
+                    out=codes.bitcast(E5X4),
+                    scales=wscales[n][:, 2 * gp + j, cols],
+                    in_=grouped[:, 1024 * j : 1024 * (j + 1)],
+                )
             return codes
 
         def mx_group(n, b):
@@ -191,7 +197,7 @@ def tile_attention_pa_kernel(tc, x, freq_cos, freq_sin, wq, wk, out_0, out_1):
             return prod
 
         def rope_sum_store(eng, n, b, prod):
-            r = rpool.tile([P, NT], F32, tag="rot")
+            r = rpool.tile([P, NT], F32, tag="rot", bufs=12)
             eng.tensor_tensor(
                 out=r[:].rearrange("p (n e) -> p n e", e=2),
                 in0=prod[:, 0, :].rearrange("p (n e) -> p n e", e=2),
@@ -207,13 +213,13 @@ def tile_attention_pa_kernel(tc, x, freq_cos, freq_sin, wq, wk, out_0, out_1):
 
         steps = [
             [("x", 0), ("x", 1)],
-            [("w", 0, 0), ("w", 0, 1)],
-            [("w", 0, 2), ("w", 0, 3)],
+            [("w", 0, 0, 0), ("w", 0, 0, 1)],
+            [("w", 0, 1, 0), ("w", 0, 1, 1)],
             [("x", 2), ("x", 3)],
         ]
         for n in range(1, N_TILES):
-            steps.append([("w", n, 0), ("w", n, 1)])
-            steps.append([("w", n, 2), ("w", n, 3)])
+            steps.append([("w", n, 0, 0), ("w", n, 0, 1)])
+            steps.append([("w", n, 1, 0), ("w", n, 1, 1)])
         n_steps = len(steps)
 
         def groups_after(s):

@@ -21,10 +21,14 @@ N_TILES = 2 * E // NT
 W_BUFS = 8
 
 
-def who_reorders(s, i):
-    if s < 4 or i == 1:
-        return None
-    return "S"
+def banks_laid_out(s, i):
+    if s < 4:
+        return 0
+    return 2 if i == 0 else 1
+
+
+def vector_banks(s, i):
+    return (1,) if s < 4 else ()
 
 
 def add_engine(s, i):
@@ -43,7 +47,7 @@ def tile_attention_pa_kernel(tc, x, freq_cos, freq_sin, wq, wk, out_0, out_1):
     with ExitStack() as ctx:
         const = ctx.enter_context(tc.tile_pool(name="const", bufs=1))
         wpool = ctx.enter_context(tc.tile_pool(name="wpool", bufs=W_BUFS))
-        opool = ctx.enter_context(tc.tile_pool(name="opool", bufs=4))
+        opool = ctx.enter_context(tc.tile_pool(name="opool", bufs=6))
         gpool = ctx.enter_context(tc.tile_pool(name="gpool", bufs=4))
         cpool = ctx.enter_context(tc.tile_pool(name="cpool", bufs=3))
         rpool = ctx.enter_context(tc.tile_pool(name="rpool", bufs=6))
@@ -102,30 +106,27 @@ def tile_attention_pa_kernel(tc, x, freq_cos, freq_sin, wq, wk, out_0, out_1):
         wscales = {}
         ordered = {}
 
-        def reorder_unit(unit, who):
+        def reorder_unit(unit, nb):
             n, rp, gp = unit[1], unit[2], unit[3]
-            re = opool.tile([P, 2, 2, 256], F32, tag="ordered")
-            src = wraw[2 * n + rp][:].bitcast(F32)[:, :, 512 * gp : 512 * (gp + 1)].rearrange(
+            re = opool.tile([P, 2, 2, P * nb], F32, tag="ordered")
+            src = wraw[2 * n + rp][:].bitcast(F32)[:, :, 512 * gp : 512 * gp + 256 * nb].rearrange(
                 "p a (w u) -> p u a w", u=2
             )
-            if who == "S":
-                nc.scalar.copy(out=re[:], in_=src)
-            else:
-                nc.vector.tensor_copy(out=re[:], in_=src)
-            ordered[unit] = re
+            nc.scalar.copy(out=re[:], in_=src)
+            ordered[unit] = (re, nb)
 
         def unit_source(unit):
-            if unit in ordered:
-                re = ordered[unit]
-                return lambda j, a, u: re[:, u, a, P * j : P * (j + 1)]
             if unit[0] == "x":
                 words = xraw[unit[1]][:].bitcast(F32)
                 return lambda j, a, u: words[:, 256 * (2 * j + a) + u : 256 * (2 * j + a + 1) : 2]
             n, rp, gp = unit[1], unit[2], unit[3]
             t = wraw[2 * n + rp]
-            return lambda j, a, u: t[:, a, :].bitcast(F32)[
-                :, 256 * (2 * gp + j) + u : 256 * (2 * gp + j + 1) : 2
-            ]
+            re, nb = ordered.get(unit, (None, 0))
+            return lambda j, a, u: (
+                re[:, u, a, P * j : P * (j + 1)]
+                if j < nb
+                else t[:, a, :].bitcast(F32)[:, 256 * (2 * gp + j) + u : 256 * (2 * gp + j + 1) : 2]
+            )
 
         def transpose_unit(unit):
             src = unit_source(unit)
@@ -139,13 +140,13 @@ def tile_attention_pa_kernel(tc, x, freq_cos, freq_sin, wq, wk, out_0, out_1):
                 banks.append(xt)
             return banks
 
-        def evacuate_unit(banks, share):
+        def evacuate_unit(banks, on_vector):
             grouped = gpool.tile([P, 2048], BF16, tag="grouped", align_bytes=64)
             gw = grouped[:].bitcast(F32)
             for j in range(2):
                 dst = gw[:, 512 * j : 512 * (j + 1)].rearrange("p (a c u) -> p a c u", a=2, u=2)
                 src = banks[j][:].rearrange("p (a u c) -> p a c u", a=2, u=2)
-                if share and j == 1:
+                if j in on_vector:
                     nc.vector.tensor_copy(out=dst, in_=src)
                 else:
                     nc.scalar.copy(out=dst, in_=src)
@@ -234,23 +235,21 @@ def tile_attention_pa_kernel(tc, x, freq_cos, freq_sin, wq, wk, out_0, out_1):
             n, pair = divmod(s - 4, 2)
             return [(n, 2 * pair), (n, 2 * pair + 1)]
 
-        def reorders(s, who):
+        def reorders(s):
             if 0 <= s < n_steps:
                 for i, unit in enumerate(steps[s]):
-                    if who_reorders(s, i) == who:
-                        reorder_unit(unit, who)
+                    if banks_laid_out(s, i):
+                        reorder_unit(unit, banks_laid_out(s, i))
 
         next_load = W_BUFS
         held = []
-        reorders(0, "S")
         for s in range(-1, n_steps + 2):
             units = steps[s] if 0 <= s < n_steps else []
             grouped = []
-            for unit in units:
+            for i, unit in enumerate(units):
                 banks = transpose_unit(unit)
-                grouped.append(evacuate_unit(banks, s < 4))
-            reorders(s + 2, "S")
-            reorders(s + 1, "V")
+                grouped.append(evacuate_unit(banks, vector_banks(s, i)))
+            reorders(s + 2)
             if units and units[0][0] == "w" and next_load < 2 * N_TILES:
                 load_w(next_load)
                 next_load += 1

@@ -24,7 +24,9 @@ W_BUFS = 8
 def banks_laid_out(s, i):
     if s < 4:
         return 0
-    return 2 if i == 0 else 1
+    if i == 0:
+        return 2
+    return 1 if s % 2 == 0 else 0
 
 
 def vector_banks(s, i):

@@ -21,12 +21,17 @@ N_TILES = 2 * E // NT
 W_BUFS = 8
 
 
+OLD_TILES = 2
+
+
 def banks_laid_out(s, i):
     if s < 4:
         return 0
     if i == 0:
         return 2
-    return 1 if s % 2 == 0 else 0
+    if s < 6:
+        return 1 if s % 2 == 0 else 0
+    return 1 if s % 2 == 1 else 0
 
 
 def vector_banks(s, i):
@@ -108,27 +113,39 @@ def tile_attention_pa_kernel(tc, x, freq_cos, freq_sin, wq, wk, out_0, out_1):
         wscales = {}
         ordered = {}
 
-        def reorder_unit(unit, nb):
-            n, rp, gp = unit[1], unit[2], unit[3]
+        def reorder_rows(n, gp, rp, nb):
             re = opool.tile([P, 2, 2, P * nb], F32, tag="ordered")
             src = wraw[2 * n + rp][:].bitcast(F32)[:, :, 512 * gp : 512 * gp + 256 * nb].rearrange(
                 "p a (w u) -> p u a w", u=2
             )
             nc.scalar.copy(out=re[:], in_=src)
-            ordered[unit] = (re, nb)
+            for j in range(nb):
+                ordered[(n, 2 * gp + j, rp)] = (re, j)
 
         def unit_source(unit):
             if unit[0] == "x":
                 words = xraw[unit[1]][:].bitcast(F32)
                 return lambda j, a, u: words[:, 256 * (2 * j + a) + u : 256 * (2 * j + a + 1) : 2]
-            n, rp, gp = unit[1], unit[2], unit[3]
-            t = wraw[2 * n + rp]
-            re, nb = ordered.get(unit, (None, 0))
-            return lambda j, a, u: (
-                re[:, u, a, P * j : P * (j + 1)]
-                if j < nb
-                else t[:, a, :].bitcast(F32)[:, 256 * (2 * gp + j) + u : 256 * (2 * gp + j + 1) : 2]
-            )
+            if unit[0] == "w":
+                n, rp, gp = unit[1], unit[2], unit[3]
+                t = wraw[2 * n + rp]
+
+                def half_source(j, a, u):
+                    re, jj = ordered.get((n, 2 * gp + j, rp), (None, 0))
+                    if re is not None:
+                        return re[:, u, a, P * jj : P * (jj + 1)]
+                    return t[:, a, :].bitcast(F32)[:, 256 * (2 * gp + j) + u : 256 * (2 * gp + j + 1) : 2]
+
+                return half_source
+            n, g = unit[1], unit[2]
+
+            def pass_source(rp, a, u):
+                re, j = ordered.get((n, g, rp), (None, 0))
+                if re is not None:
+                    return re[:, u, a, P * j : P * (j + 1)]
+                return wraw[2 * n + rp][:, a, :].bitcast(F32)[:, 256 * g + u : 256 * (g + 1) : 2]
+
+            return pass_source
 
         def transpose_unit(unit):
             src = unit_source(unit)
@@ -160,6 +177,16 @@ def tile_attention_pa_kernel(tc, x, freq_cos, freq_sin, wq, wk, out_0, out_1):
                 nc.vector.quantize_mx(
                     out=codes.bitcast(E5X4), scales=xscales[:, unit[1], :], in_=grouped[:]
                 )
+                return codes
+            if unit[0] == "g":
+                n, g = unit[1], unit[2]
+                if g == 0:
+                    wc = cpool.tile([P, PASSES, NT], U32, tag="wcodes", align_bytes=64)
+                    ws = cpool.tile([P, PASSES, NT], U8, tag="wscales", align_bytes=64)
+                    wcodes[n] = wc
+                    wscales[n] = ws
+                codes = wcodes[n][:, g, :]
+                nc.vector.quantize_mx(out=codes.bitcast(E5X4), scales=wscales[n][:, g, :], in_=grouped[:])
                 return codes
             n, rp, gp = unit[1], unit[2], unit[3]
             if rp == 0 and gp == 0:
@@ -220,9 +247,12 @@ def tile_attention_pa_kernel(tc, x, freq_cos, freq_sin, wq, wk, out_0, out_1):
             [("w", 0, 1, 0), ("w", 0, 1, 1)],
             [("x", 2), ("x", 3)],
         ]
-        for n in range(1, N_TILES):
+        for n in range(1, OLD_TILES):
             steps.append([("w", n, 0, 0), ("w", n, 0, 1)])
             steps.append([("w", n, 1, 0), ("w", n, 1, 1)])
+        for n in range(OLD_TILES, N_TILES):
+            steps.append([("g", n, 0), ("g", n, 1)])
+            steps.append([("g", n, 2), ("g", n, 3)])
         n_steps = len(steps)
 
         def groups_after(s):
@@ -238,10 +268,14 @@ def tile_attention_pa_kernel(tc, x, freq_cos, freq_sin, wq, wk, out_0, out_1):
             return [(n, 2 * pair), (n, 2 * pair + 1)]
 
         def reorders(s):
-            if 0 <= s < n_steps:
+            if 0 <= s < n_steps and steps[s][0][0] == "w":
                 for i, unit in enumerate(steps[s]):
                     if banks_laid_out(s, i):
-                        reorder_unit(unit, banks_laid_out(s, i))
+                        reorder_rows(unit[1], unit[3], unit[2], banks_laid_out(s, i))
+            if 0 <= s < n_steps and steps[s][0][0] == "g":
+                for rp in range(2):
+                    if banks_laid_out(s, rp):
+                        reorder_rows(steps[s][0][1], steps[s][0][2] // 2, rp, banks_laid_out(s, rp))
 
         next_load = W_BUFS
         held = []
@@ -255,6 +289,10 @@ def tile_attention_pa_kernel(tc, x, freq_cos, freq_sin, wq, wk, out_0, out_1):
             if units and units[0][0] == "w" and next_load < 2 * N_TILES:
                 load_w(next_load)
                 next_load += 1
+            if units and units[0][0] == "g" and units[0][2] == 2 and next_load < 2 * N_TILES:
+                load_w(next_load)
+                load_w(next_load + 1)
+                next_load += 2
             groups = groups_after(s)
             accs = [mx_group(n, b) for (n, b) in groups]
             codes = None

@@ -29,9 +29,9 @@ def banks_laid_out(s, i):
         return 0
     if i == 0:
         return 2
-    if s < 6:
-        return 1 if s % 2 == 0 else 0
-    return 1 if s % 2 == 1 else 0
+    if s < 7:
+        return 1 if s == 4 else 0
+    return 1
 
 
 def vector_banks(s, i):
@@ -54,7 +54,7 @@ def tile_attention_pa_kernel(tc, x, freq_cos, freq_sin, wq, wk, out_0, out_1):
     with ExitStack() as ctx:
         const = ctx.enter_context(tc.tile_pool(name="const", bufs=1))
         wpool = ctx.enter_context(tc.tile_pool(name="wpool", bufs=W_BUFS))
-        opool = ctx.enter_context(tc.tile_pool(name="opool", bufs=6))
+        opool = ctx.enter_context(tc.tile_pool(name="opool", bufs=8))
         gpool = ctx.enter_context(tc.tile_pool(name="gpool", bufs=4))
         cpool = ctx.enter_context(tc.tile_pool(name="cpool", bufs=3))
         rpool = ctx.enter_context(tc.tile_pool(name="rpool", bufs=6))

@@ -41,8 +41,6 @@ def vector_banks(s, i):
 def add_engine(s, i):
     if s == 19:
         return "V"
-    if s == 18:
-        return "G"
     return "V" if i == 0 else "G"
 
 
@@ -285,7 +283,10 @@ def tile_attention_pa_kernel(tc, x, freq_cos, freq_sin, wq, wk, out_0, out_1):
             for i, unit in enumerate(units):
                 banks = transpose_unit(unit)
                 grouped.append(evacuate_unit(banks, vector_banks(s, i)))
-            reorders(s + 2)
+            if s == 3:
+                reorders(4)
+            if s + 2 > 4:
+                reorders(s + 2)
             if units and units[0][0] == "w" and next_load < 2 * N_TILES:
                 load_w(next_load)
                 next_load += 1

@@ -18,7 +18,7 @@ P = 128
 NT = 512
 PASSES = D // 512
 N_TILES = 2 * E // NT
-W_BUFS = 8
+W_BUFS = 6
 
 
 OLD_TILES = 2
@@ -87,13 +87,18 @@ def tile_attention_pa_kernel(tc, x, freq_cos, freq_sin, wq, wk, out_0, out_1):
             nc.sync.dma_start(out=t[:], in_=w[r0 : r0 + 256, :].rearrange("(a p) k -> p a k", p=P))
             wraw[q] = t
 
+        def load_rows(rb):
+            t = const.tile([P, D], BF16, name="wrow%d" % rb)
+            nc.sync.dma_start(out=t[:], in_=wq[P * rb : P * (rb + 1), :])
+            wraw[("r", rb)] = t
+
         load_x(0)
         load_x(1)
-        load_w(0)
-        load_w(1)
+        for rb in range(4):
+            load_rows(rb)
         load_x(2)
         load_x(3)
-        for q in range(2, W_BUFS):
+        for q in range(2, 2 + W_BUFS):
             load_w(q)
 
         table = const.tile([P, 2, NT], F32, name="table")
@@ -124,6 +129,9 @@ def tile_attention_pa_kernel(tc, x, freq_cos, freq_sin, wq, wk, out_0, out_1):
             if unit[0] == "x":
                 words = xraw[unit[1]][:].bitcast(F32)
                 return lambda j, a, u: words[:, 256 * (2 * j + a) + u : 256 * (2 * j + a + 1) : 2]
+            if unit[0] == "r":
+                rows = wraw[unit][:].bitcast(F32)
+                return lambda j, a, u: rows[:, 256 * (2 * j + a) + u : 256 * (2 * j + a + 1) : 2]
             if unit[0] == "w":
                 n, rp, gp = unit[1], unit[2], unit[3]
                 t = wraw[2 * n + rp]
@@ -175,6 +183,20 @@ def tile_attention_pa_kernel(tc, x, freq_cos, freq_sin, wq, wk, out_0, out_1):
                 nc.vector.quantize_mx(
                     out=codes.bitcast(E5X4), scales=xscales[:, unit[1], :], in_=grouped[:]
                 )
+                return codes
+            if unit[0] == "r":
+                rb = unit[1]
+                if rb == 0:
+                    wc = cpool.tile([P, PASSES, NT], U32, tag="wcodes", align_bytes=64)
+                    ws = cpool.tile([P, PASSES, NT], U8, tag="wscales", align_bytes=64)
+                    wcodes[0] = wc
+                    wscales[0] = ws
+                cols = slice(P * rb, P * (rb + 1))
+                for g in range(PASSES):
+                    codes = wcodes[0][:, g, cols]
+                    nc.vector.quantize_mx(
+                        out=codes.bitcast(E5X4), scales=wscales[0][:, g, cols], in_=grouped[:, 512 * g : 512 * (g + 1)]
+                    )
                 return codes
             if unit[0] == "g":
                 n, g = unit[1], unit[2]
@@ -241,8 +263,8 @@ def tile_attention_pa_kernel(tc, x, freq_cos, freq_sin, wq, wk, out_0, out_1):
 
         steps = [
             [("x", 0), ("x", 1)],
-            [("w", 0, 0, 0), ("w", 0, 0, 1)],
-            [("w", 0, 1, 0), ("w", 0, 1, 1)],
+            [("r", 0), ("r", 1)],
+            [("r", 2), ("r", 3)],
             [("x", 2), ("x", 3)],
         ]
         for n in range(1, OLD_TILES):
@@ -275,7 +297,7 @@ def tile_attention_pa_kernel(tc, x, freq_cos, freq_sin, wq, wk, out_0, out_1):
                     if banks_laid_out(s, rp):
                         reorder_rows(steps[s][0][1], steps[s][0][2] // 2, rp, banks_laid_out(s, rp))
 
-        next_load = W_BUFS
+        next_load = 2 + W_BUFS
         held = []
         for s in range(-1, n_steps + 2):
             units = steps[s] if 0 <= s < n_steps else []

@@ -25,7 +25,7 @@ OLD_TILES = 2
 
 
 def banks_laid_out(s, i):
-    if s < 4:
+    if s < 4 or s == 5:
         return 0
     if i == 0:
         return 2

from contextlib import ExitStack

import concourse.mybir as mybir
from concourse.masks import make_identity

B, S, D, H, HD = 4, 128, 2048, 16, 128
E = H * HD
HALF = HD // 2
FLOPS = 2 * (B * S) * D * (2 * E)

F32 = mybir.dt.float32
BF16 = mybir.dt.bfloat16
U32 = mybir.dt.uint32
U8 = mybir.dt.uint8
E5X4 = mybir.dt.float8_e5m2_x4

P = 128
NT = 512
PASSES = D // 512
N_TILES = 2 * E // NT
W_BUFS = 6


OLD_TILES = 2


def banks_laid_out(s, i):
    if s < 4 or s == 5:
        return 0
    if i == 0:
        return 2
    if s < 7:
        return 1 if s == 4 else 0
    return 1


def vector_banks(s, i):
    return (1,) if s < 4 else ()


def add_engine(s, i):
    if s == 19:
        return "V"
    return "V" if i == 0 else "G"


def tile_attention_pa_kernel(tc, x, freq_cos, freq_sin, wq, wk, out_0, out_1):
    nc = tc.nc
    mult = mybir.AluOpType.mult
    add = mybir.AluOpType.add

    with ExitStack() as ctx:
        const = ctx.enter_context(tc.tile_pool(name="const", bufs=1))
        wpool = ctx.enter_context(tc.tile_pool(name="wpool", bufs=W_BUFS))
        opool = ctx.enter_context(tc.tile_pool(name="opool", bufs=8))
        gpool = ctx.enter_context(tc.tile_pool(name="gpool", bufs=4))
        cpool = ctx.enter_context(tc.tile_pool(name="cpool", bufs=3))
        rpool = ctx.enter_context(tc.tile_pool(name="rpool", bufs=6))
        tpsum = ctx.enter_context(tc.psum_pool(name="tpsum", bufs=4))
        mpsum = ctx.enter_context(tc.psum_pool(name="mpsum", bufs=4))
        ctx.enter_context(tc.manual_schedule())

        cos_raw = const.tile([P, HALF], BF16, name="cos_raw")
        sin_raw = const.tile([P, HALF], BF16, name="sin_raw")
        nc.scalar.dma_start(out=cos_raw[:], in_=freq_cos[:, :])
        nc.scalar.dma_start(out=sin_raw[:], in_=freq_sin[:, :])

        ident = const.tile([P, P], F32, name="ident")
        make_identity(nc, ident[:])
        junk = const.tile([P, 1], U32, name="junk")
        warm = const.tile([P, 1], F32, name="warm")
        nc.scalar.copy(out=warm[:], in_=ident[:, 0:1])

        xraw = {}
        wraw = {}

        def load_x(b):
            t = const.tile([P, D], BF16, name="xraw%d" % b)
            nc.sync.dma_start(out=t[:], in_=x[b, :, :])
            xraw[b] = t

        def load_w(q):
            n, rp = divmod(q, 2)
            w = wq if n < N_TILES // 2 else wk
            r0 = (n % (N_TILES // 2)) * NT + 256 * rp
            t = wpool.tile([P, 2, D], BF16, tag="wraw")
            nc.sync.dma_start(out=t[:], in_=w[r0 : r0 + 256, :].rearrange("(a p) k -> p a k", p=P))
            wraw[q] = t

        def load_rows(rb):
            t = const.tile([P, D], BF16, name="wrow%d" % rb)
            nc.sync.dma_start(out=t[:], in_=wq[P * rb : P * (rb + 1), :])
            wraw[("r", rb)] = t

        load_x(0)
        load_x(1)
        for rb in range(4):
            load_rows(rb)
        load_x(2)
        load_x(3)
        for q in range(2, 2 + W_BUFS):
            load_w(q)

        table = const.tile([P, 2, NT], F32, name="table")
        sin2v = table[:, 1, :].rearrange("p (h j e) -> p h j e", h=4, e=2)
        nc.scalar.copy(
            out=table[:, 0, :].rearrange("p (h j e) -> p h j e", h=4, e=2),
            in_=cos_raw[:].unsqueeze(1).unsqueeze(3).to_broadcast([P, 4, HALF, 2]),
        )
        nc.scalar.copy(out=sin2v[:, :, :, 0], in_=sin_raw[:].unsqueeze(1).to_broadcast([P, 4, HALF]))
        nc.scalar.mul(out=sin2v[:, :, :, 1], in_=sin_raw[:].unsqueeze(1).to_broadcast([P, 4, HALF]), mul=-1.0)

        xcodes = const.tile([P, B, 512], U32, name="xcodes", align_bytes=64)
        xscales = const.tile([P, B, 512], U8, name="xscales", align_bytes=64)
        wcodes = {}
        wscales = {}
        ordered = {}

        def reorder_rows(n, gp, rp, nb):
            re = opool.tile([P, 2, 2, P * nb], F32, tag="ordered")
            src = wraw[2 * n + rp][:].bitcast(F32)[:, :, 512 * gp : 512 * gp + 256 * nb].rearrange(
                "p a (w u) -> p u a w", u=2
            )
            nc.scalar.copy(out=re[:], in_=src)
            for j in range(nb):
                ordered[(n, 2 * gp + j, rp)] = (re, j)

        def unit_source(unit):
            if unit[0] == "x":
                words = xraw[unit[1]][:].bitcast(F32)
                return lambda j, a, u: words[:, 256 * (2 * j + a) + u : 256 * (2 * j + a + 1) : 2]
            if unit[0] == "r":
                rows = wraw[unit][:].bitcast(F32)
                return lambda j, a, u: rows[:, 256 * (2 * j + a) + u : 256 * (2 * j + a + 1) : 2]
            if unit[0] == "w":
                n, rp, gp = unit[1], unit[2], unit[3]
                t = wraw[2 * n + rp]

                def half_source(j, a, u):
                    re, jj = ordered.get((n, 2 * gp + j, rp), (None, 0))
                    if re is not None:
                        return re[:, u, a, P * jj : P * (jj + 1)]
                    return t[:, a, :].bitcast(F32)[:, 256 * (2 * gp + j) + u : 256 * (2 * gp + j + 1) : 2]

                return half_source
            n, g = unit[1], unit[2]

            def pass_source(rp, a, u):
                re, j = ordered.get((n, g, rp), (None, 0))
                if re is not None:
                    return re[:, u, a, P * j : P * (j + 1)]
                return wraw[2 * n + rp][:, a, :].bitcast(F32)[:, 256 * g + u : 256 * (g + 1) : 2]

            return pass_source

        def transpose_unit(unit):
            src = unit_source(unit)
            banks = []
            for j in range(2):
                xt = tpsum.tile([P, 512], F32, tag="xt")
                for a in range(2):
                    for u in range(2):
                        c = (2 * a + u) * P
                        nc.tensor.transpose(xt[:, c : c + P], src(j, a, u), ident[:])
                banks.append(xt)
            return banks

        def evacuate_unit(banks, on_vector):
            grouped = gpool.tile([P, 2048], BF16, tag="grouped", align_bytes=64)
            gw = grouped[:].bitcast(F32)
            for j in range(2):
                dst = gw[:, 512 * j : 512 * (j + 1)].rearrange("p (a c u) -> p a c u", a=2, u=2)
                src = banks[j][:].rearrange("p (a u c) -> p a c u", a=2, u=2)
                if j in on_vector:
                    nc.vector.tensor_copy(out=dst, in_=src)
                else:
                    nc.scalar.copy(out=dst, in_=src)
            return grouped

        def quantize_unit(unit, grouped):
            if unit[0] == "x":
                codes = xcodes[:, unit[1], :]
                nc.vector.quantize_mx(
                    out=codes.bitcast(E5X4), scales=xscales[:, unit[1], :], in_=grouped[:]
                )
                return codes
            if unit[0] == "r":
                rb = unit[1]
                if rb == 0:
                    wc = cpool.tile([P, PASSES, NT], U32, tag="wcodes", align_bytes=64)
                    ws = cpool.tile([P, PASSES, NT], U8, tag="wscales", align_bytes=64)
                    wcodes[0] = wc
                    wscales[0] = ws
                cols = slice(P * rb, P * (rb + 1))
                for g in range(PASSES):
                    codes = wcodes[0][:, g, cols]
                    nc.vector.quantize_mx(
                        out=codes.bitcast(E5X4), scales=wscales[0][:, g, cols], in_=grouped[:, 512 * g : 512 * (g + 1)]
                    )
                return codes
            if unit[0] == "g":
                n, g = unit[1], unit[2]
                if g == 0:
                    wc = cpool.tile([P, PASSES, NT], U32, tag="wcodes", align_bytes=64)
                    ws = cpool.tile([P, PASSES, NT], U8, tag="wscales", align_bytes=64)
                    wcodes[n] = wc
                    wscales[n] = ws
                codes = wcodes[n][:, g, :]
                nc.vector.quantize_mx(out=codes.bitcast(E5X4), scales=wscales[n][:, g, :], in_=grouped[:])
                return codes
            n, rp, gp = unit[1], unit[2], unit[3]
            if rp == 0 and gp == 0:
                wc = cpool.tile([P, PASSES, NT], U32, tag="wcodes", align_bytes=64)
                ws = cpool.tile([P, PASSES, NT], U8, tag="wscales", align_bytes=64)
                wcodes[n] = wc
                wscales[n] = ws
            cols = slice(256 * rp, 256 * (rp + 1))
            for j in range(2):
                codes = wcodes[n][:, 2 * gp + j, cols]
                nc.vector.quantize_mx(
                    out=codes.bitcast(E5X4),
                    scales=wscales[n][:, 2 * gp + j, cols],
                    in_=grouped[:, 1024 * j : 1024 * (j + 1)],
                )
            return codes

        def mx_group(n, b):
            acc = mpsum.tile([P, NT], F32, tag="acc")
            for g in range(PASSES):
                cols = slice(P * g, P * (g + 1))
                nc.tensor.matmul_mx(
                    out=acc[:],
                    lhsT=xcodes[:, b, cols].bitcast(E5X4),
                    lhsT_scale=xscales[:, b, cols],
                    rhs=wcodes[n][:, g, :].bitcast(E5X4),
                    rhs_scale=wscales[n][:, g, :],
                    start=(g == 0),
                    stop=(g == PASSES - 1),
                )
            return acc

        def rope_products(acc):
            prod = rpool.tile([P, 2, NT], F32, tag="prod")
            nc.vector.tensor_tensor(
                out=prod[:], in0=acc[:].unsqueeze(1).to_broadcast([P, 2, NT]), in1=table[:], op=mult
            )
            return prod

        def rope_sum_store(eng, n, b, prod):
            r = rpool.tile([P, NT], F32, tag="rot", bufs=12)
            eng.tensor_tensor(
                out=r[:].rearrange("p (n e) -> p n e", e=2),
                in0=prod[:, 0, :].rearrange("p (n e) -> p n e", e=2),
                in1=prod[:, 1, :].rearrange("p (n e) -> p n e", e=2)[:, :, ::-1],
                op=add,
            )
            dst = out_0 if n < N_TILES // 2 else out_1
            h0 = (n % (N_TILES // 2)) * 4
            nc.sync.dma_start(
                out=dst[b, h0 : h0 + 4, :, :].rearrange("h s f -> s h f"),
                in_=r[:].rearrange("p (h f) -> p h f", h=4),
            )

        steps = [
            [("x", 0), ("x", 1)],
            [("r", 0), ("r", 1)],
            [("r", 2), ("r", 3)],
            [("x", 2), ("x", 3)],
        ]
        for n in range(1, OLD_TILES):
            steps.append([("w", n, 0, 0), ("w", n, 0, 1)])
            steps.append([("w", n, 1, 0), ("w", n, 1, 1)])
        for n in range(OLD_TILES, N_TILES):
            steps.append([("g", n, 0), ("g", n, 1)])
            steps.append([("g", n, 2), ("g", n, 3)])
        n_steps = len(steps)

        def groups_after(s):
            if s < 3:
                return []
            if s == 3:
                return [(0, 0), (0, 1)]
            if s == 4:
                return [(0, 2)]
            if s == 5:
                return [(0, 3)]
            n, pair = divmod(s - 4, 2)
            return [(n, 2 * pair), (n, 2 * pair + 1)]

        def reorders(s):
            if 0 <= s < n_steps and steps[s][0][0] == "w":
                for i, unit in enumerate(steps[s]):
                    if banks_laid_out(s, i):
                        reorder_rows(unit[1], unit[3], unit[2], banks_laid_out(s, i))
            if 0 <= s < n_steps and steps[s][0][0] == "g":
                for rp in range(2):
                    if banks_laid_out(s, rp):
                        reorder_rows(steps[s][0][1], steps[s][0][2] // 2, rp, banks_laid_out(s, rp))

        next_load = 2 + W_BUFS
        held = []
        for s in range(-1, n_steps + 2):
            units = steps[s] if 0 <= s < n_steps else []
            grouped = []
            for i, unit in enumerate(units):
                banks = transpose_unit(unit)
                grouped.append(evacuate_unit(banks, vector_banks(s, i)))
            if s == 3:
                reorders(4)
            if s + 2 > 4:
                reorders(s + 2)
            if units and units[0][0] == "w" and next_load < 2 * N_TILES:
                load_w(next_load)
                next_load += 1
            if units and units[0][0] == "g" and units[0][2] == 2 and next_load < 2 * N_TILES:
                load_w(next_load)
                load_w(next_load + 1)
                next_load += 2
            groups = groups_after(s)
            accs = [mx_group(n, b) for (n, b) in groups]
            codes = None
            for unit, gr in zip(units, grouped):
                codes = quantize_unit(unit, gr)
            if codes is not None and held:
                nc.gpsimd.tensor_copy(out=junk[:], in_=codes[:, 0:1])
            for (n, b), pr in held:
                rope_sum_store(nc.gpsimd, n, b, pr)
            held = []
            prods = [rope_products(acc) for acc in accs]
            for i, ((n, b), pr) in enumerate(zip(groups, prods)):
                if add_engine(s, i) == "V":
                    rope_sum_store(nc.vector, n, b, pr)
                else:
                    held.append(((n, b), pr))
            if s >= n_steps - 1:
                for (n, b), pr in held:
                    rope_sum_store(nc.gpsimd, n, b, pr)
                held = []
